import numpy as np
import ml_dtypes


def mxq(x, axis, fmt="e4m3"):
    dtype, down = {"e4m3": (ml_dtypes.float8_e4m3fn, 7), "e5m2": (ml_dtypes.float8_e5m2, 14)}[fmt]
    v = np.moveaxis(np.asarray(x, np.float32).astype(ml_dtypes.bfloat16).astype(np.float64), axis, -1)
    blocks = v.reshape(v.shape[:-1] + (-1, 32))
    amax = np.abs(blocks).max(-1, keepdims=True)
    byte = np.maximum(np.where(amax > 0, np.frexp(amax)[1] - 1 + 127, 0) - down, 1)
    scale = np.exp2(byte - 127.0)
    codes = (blocks / scale).astype(np.float32).astype(dtype).astype(np.float64)
    return np.moveaxis((codes * scale).reshape(v.shape), -1, axis)


WIDE = False


def mx_kscale(k):
    if not WIDE:
        return np.ones(k)
    levels = np.array([10, -10, 5, -5, 0])
    a = np.random.permutation(np.resize(levels, k // 512 * 4)).reshape(k // 512, 4)
    idx = np.arange(k)
    return np.exp2(a[idx // 512, idx % 128 // 32])


BF16 = ml_dtypes.bfloat16


def bf(x):
    return np.asarray(x, np.float32).astype(BF16)


def f64(x):
    return np.asarray(x).astype(np.float64)


B, D_IN, D_OUT = 4096, 512, 512


def sigmoid(v):
    return 1.0 / (1.0 + np.exp(-v))


def setup_inputs():
    s, t = mx_kscale(D_IN), mx_kscale(D_OUT)

    def wx():
        return bf(np.random.standard_normal((D_IN, D_OUT)) / np.sqrt(D_IN) / s[:, None])

    def wh():
        return bf(np.random.standard_normal((D_OUT, D_OUT)) / np.sqrt(D_OUT) / t[:, None])

    return {"x": bf(np.random.standard_normal((B, D_IN)) * s),
            "hist": bf(np.random.standard_normal((B, D_OUT)) * t),
            "ig": bf(np.random.standard_normal((B, D_OUT)) * 0.4),
            "carousel": bf(np.random.uniform(1.25, 1.75, 1)),
            "Wfx": wx(), "Wfh": wh(), "b_f": bf(np.random.standard_normal(D_OUT) * 0.3),
            "Wox": wx(), "Woh": wh(), "b_o": bf(np.random.standard_normal(D_OUT) * 0.3)}


def reference(x, hist, ig, carousel, Wfx, Wfh, b_f, Wox, Woh, b_o):
    xq = mxq(f64(x), 1, "e4m3")
    hq = mxq(f64(hist), 1, "e4m3")
    f = sigmoid((xq @ mxq(f64(Wfx), 0, "e4m3")) + (hq @ mxq(f64(Wfh), 0, "e4m3")) + f64(b_f))
    o = sigmoid((xq @ mxq(f64(Wox), 0, "e4m3")) + (hq @ mxq(f64(Woh), 0, "e4m3")) + f64(b_o))
    c = f * f64(carousel) + f64(ig)
    h = o * c
    return (h, c)

@@ -1,0 +1,293 @@
+from contextlib import ExitStack
+
+import concourse.mybir as mybir
+from concourse.masks import make_identity
+
+F32 = mybir.dt.float32
+BF16 = mybir.dt.bfloat16
+U32 = mybir.dt.uint32
+U8 = mybir.dt.uint8
+FP8X4 = mybir.dt.float8_e4m3fn_x4
+ACT = mybir.ActivationFunctionType
+ALU = mybir.AluOpType
+
+P = 128
+B = 4096
+D = 512
+GROUP = 512
+TILES = GROUP // P
+NG = B // GROUP
+FLOPS = 4 * 2 * B * D * D
+
+S_COLS = 160
+
+
+def tile_lstmmirrored_pb_t_kernel(
+    tc, x, hist, ig, carousel, Wfx, Wfh, b_f, Wox, Woh, b_o, out_0, out_1
+):
+    nc = tc.nc
+    with ExitStack() as ctx:
+        ctx.enter_context(tc.manual_schedule())
+        const = ctx.enter_context(tc.tile_pool(name="const", bufs=1))
+        wstage = ctx.enter_context(tc.tile_pool(name="wstage", bufs=1))
+        acts = ctx.enter_context(tc.tile_pool(name="acts", bufs=4))
+        igp = ctx.enter_context(tc.tile_pool(name="igp", bufs=5))
+        work = ctx.enter_context(tc.tile_pool(name="work", bufs=2))
+        outp = ctx.enter_context(tc.tile_pool(name="outp", bufs=3))
+        psum = ctx.enter_context(tc.psum_pool(name="psum", bufs=8))
+
+        def bank(name):
+            return psum.tile([P, 512], F32, name=name, tag="bank")
+
+        def rows(ap, g):
+            return ap[g * GROUP : (g + 1) * GROUP, :].rearrange("(p t) d -> p t d", t=TILES)
+
+        x_sb = {}
+        h_sb = {}
+        ig_sb = {}
+
+        def load_acts(g):
+            x_sb[g] = acts.tile([P, TILES, D], BF16, name="x_sb", tag="x")
+            nc.sync.dma_start(out=x_sb[g][:], in_=rows(x, g))
+            h_sb[g] = acts.tile([P, TILES, D], BF16, name="h_sb", tag="h")
+            nc.sync.dma_start(out=h_sb[g][:], in_=rows(hist, g))
+
+        def load_ig(g):
+            ig_sb[g] = igp.tile([P, TILES, D], BF16, name="ig_sb", tag="ig")
+            nc.sync.dma_start(out=ig_sb[g][:], in_=rows(ig, g))
+
+        weights = [Wfx, Wfh, Wox, Woh]
+        wraw = []
+
+        def load_w(w):
+            t = wstage.tile([P, 4, D], BF16, name="wraw%d" % w)
+            nc.sync.dma_start(
+                out=t[:].rearrange("p (u e) c -> p u e c", u=2),
+                in_=weights[w].rearrange("(u q e) c -> q u e c", u=2, e=2),
+            )
+            wraw.append(t)
+
+        ones = const.tile([P, P], BF16, name="ones")
+        nc.vector.memset(ones[:], 1.0)
+        brow = const.tile([P, D], BF16, name="brow")
+        nc.vector.memset(brow[:], 0.0)
+        bft = const.tile([P, P], BF16, name="bft")
+        nc.vector.memset(bft[:], 0.0)
+        warm = const.tile([P, 1], F32, name="warm")
+        nc.vector.memset(warm[:], 0.0)
+        car_bf = const.tile([P, 1], BF16, name="car_bf")
+        nc.scalar.dma_start(out=brow[0:1, :], in_=b_o.unsqueeze(0))
+        nc.scalar.dma_start(out=bft[0:4, :], in_=b_f.rearrange("(m d) -> m d", m=4))
+        nc.scalar.dma_start(out=car_bf[:], in_=carousel.partition_broadcast(P))
+        nc.scalar.activation(out=warm[:], in_=warm[:], func=ACT.Sigmoid)
+
+        ident = const.tile([P, P], F32, name="ident")
+        make_identity(nc, ident[:])
+        ident_bf = const.tile([P, P], BF16, name="ident_bf")
+        make_identity(nc, ident_bf[:])
+
+        load_w(0)
+        load_w(1)
+        load_acts(0)
+        load_w(2)
+        load_w(3)
+        load_acts(1)
+        load_ig(0)
+        load_acts(2)
+        load_ig(1)
+        load_acts(3)
+        load_ig(2)
+
+        bo_ps = bank("bo_ps")
+        nc.tensor.matmul(out=bo_ps[:], lhsT=ones[:], rhs=brow[:], start=True, stop=True)
+        bf_ps = bank("bf_ps")
+        nc.tensor.matmul(out=bf_ps[:, 0:32], lhsT=bft[:], rhs=ident_bf[:, 0:32], start=True, stop=True)
+
+        wcodes = const.tile([P, 4, D], U32, name="wcodes", align_bytes=64)
+        wscales = const.tile([P, 4, D], U8, name="wscales", align_bytes=64)
+        wgrp = {}
+
+        def regroup_w(w, s_cols):
+            wgrp[w] = wstage.tile([P, D, 4], BF16, name="wgrp%d" % w, align_bytes=64)
+            v_cols = D - s_cols
+            nc.vector.tensor_copy(
+                out=wgrp[w][:, 0:v_cols, :].rearrange("p (c i) t -> p c t i", i=4),
+                in_=wraw[w][:, :, 0:v_cols].rearrange("p t (c i) -> p c t i", i=4),
+            )
+            if s_cols:
+                nc.scalar.copy(
+                    out=wgrp[w][:, v_cols:D, :].rearrange("p (c i) t -> p c t i", i=4),
+                    in_=wraw[w][:, :, v_cols:D].rearrange("p t (c i) -> p c t i", i=4),
+                )
+
+        def quant_w(w):
+            nc.vector.quantize_mx(
+                out=wcodes[:, w, :].bitcast(FP8X4),
+                scales=wscales[:, w, :],
+                in_=wgrp[w][:].rearrange("p c t -> p (c t)"),
+            )
+
+        bo_bc = const.tile([P, D], F32, name="bo_bc")
+        bf_col = const.tile([P, 4], F32, name="bf_col")
+        car = const.tile([P, 1], F32, name="car")
+
+        regroup_w(0, S_COLS)
+        nc.vector.tensor_copy(out=bo_bc[:], in_=bo_ps[:])
+        nc.vector.tensor_copy(out=bf_col[:], in_=bf_ps[:, 0:4])
+        nc.vector.tensor_copy(out=car[:], in_=car_bf[:])
+        quant_w(0)
+        regroup_w(1, S_COLS)
+
+        grp = {}
+        codes = {}
+        scales = {}
+        fT = {}
+        o_sb = {}
+        c_sb = {}
+        hh_sb = {}
+
+        def stage_in(g, k):
+            op, j = k // 2, k % 2
+            if k == 0:
+                grp[g] = work.tile([P, 2, 4 * GROUP], BF16, name="grp", tag="grp", align_bytes=64)
+            src = (x_sb[g], h_sb[g])[op]
+            ps = bank("in_ps")
+            for tt in range(2):
+                words = src[:, 2 * j + tt, :].bitcast(F32)
+                for u in range(2):
+                    nc.tensor.transpose(
+                        out=ps[:, u * 256 + tt * P : u * 256 + (tt + 1) * P],
+                        in_=words[:, u * P : (u + 1) * P],
+                        identity=ident[:],
+                    )
+            nc.scalar.copy(
+                out=grp[g][:, op, :].bitcast(F32)[:, j * 512 : (j + 1) * 512].rearrange(
+                    "p (n u) -> p n u", u=2
+                ),
+                in_=ps[:].rearrange("p (u n) -> p n u", u=2),
+            )
+
+        def quant(g, op):
+            if op == 0:
+                codes[g] = work.tile([P, 2, GROUP], U32, name="codes", tag="codes", align_bytes=64)
+                scales[g] = work.tile([P, 2, GROUP], U8, name="scales", tag="scales", align_bytes=64)
+            nc.vector.quantize_mx(
+                out=codes[g][:, op, :].bitcast(FP8X4),
+                scales=scales[g][:, op, :],
+                in_=grp[g][:, op, :],
+            )
+
+        def stage_f(g, m):
+            if m == 0:
+                fT[g] = work.tile([P, 4, GROUP], F32, name="fT", tag="fT")
+            ps = bank("f_ps")
+            cols = slice(m * P, (m + 1) * P)
+            for op in range(2):
+                nc.tensor.matmul_mx(
+                    out=ps[:],
+                    lhsT=wcodes[:, op, cols].bitcast(FP8X4),
+                    lhsT_scale=wscales[:, op, cols],
+                    rhs=codes[g][:, op, :].bitcast(FP8X4),
+                    rhs_scale=scales[g][:, op, :],
+                    start=(op == 0),
+                    stop=(op == 1),
+                )
+            nc.scalar.activation(
+                out=fT[g][:, m, :], in_=ps[:], func=ACT.Sigmoid, bias=bf_col[:, m : m + 1], scale=1.0
+            )
+
+        def stage_o(g, t):
+            if t == 0:
+                o_sb[g] = work.tile([P, TILES, D], F32, name="o_sb", tag="o")
+            ps = bank("o_ps")
+            cols = slice(t * P, (t + 1) * P)
+            for op in range(2):
+                nc.tensor.matmul_mx(
+                    out=ps[:],
+                    lhsT=codes[g][:, op, cols].bitcast(FP8X4),
+                    lhsT_scale=scales[g][:, op, cols],
+                    rhs=wcodes[:, 2 + op, :].bitcast(FP8X4),
+                    rhs_scale=wscales[:, 2 + op, :],
+                    start=(op == 0),
+                    stop=(op == 1),
+                )
+            nc.vector.tensor_tensor(out=o_sb[g][:, t, :], in0=ps[:], in1=bo_bc[:], op=ALU.add)
+            nc.scalar.activation(out=o_sb[g][:, t, :], in_=o_sb[g][:, t, :], func=ACT.Sigmoid)
+
+        def stage_back(g, t):
+            if t == 0:
+                c_sb[g] = outp.tile([P, TILES, D], F32, name="c_sb", tag="c")
+                hh_sb[g] = outp.tile([P, TILES, D], F32, name="hh_sb", tag="hh")
+            ps = bank("b_ps")
+            for m in range(4):
+                nc.tensor.transpose(
+                    out=ps[:, m * P : (m + 1) * P],
+                    in_=fT[g][:, m, t * P : (t + 1) * P],
+                    identity=ident[:],
+                )
+            nc.vector.scalar_tensor_tensor(
+                out=c_sb[g][:, t, :],
+                in0=ps[:],
+                scalar=car[:, 0:1],
+                in1=ig_sb[g][:, t, :],
+                op0=ALU.mult,
+                op1=ALU.add,
+            )
+
+        def stage_h(g, t, eng):
+            eng.tensor_tensor(
+                out=hh_sb[g][:, t, :], in0=o_sb[g][:, t, :], in1=c_sb[g][:, t, :], op=ALU.mult
+            )
+
+        for g in range(NG):
+            last = g == NG - 1
+            if g == 0:
+                for k in range(4):
+                    stage_in(0, k)
+                    if k == 1:
+                        quant_w(1)
+                        quant(0, 0)
+                        regroup_w(2, 0)
+                quant(0, 1)
+                quant_w(2)
+                regroup_w(3, 0)
+                quant_w(3)
+            else:
+                if g == 1:
+                    for k in range(4):
+                        stage_in(1, k)
+                    quant(1, 0)
+                    quant(1, 1)
+                for k in range(4):
+                    if g + 1 < NG:
+                        stage_in(g + 1, k)
+                    stage_back(g - 1, k)
+                    stage_h(g - 1, k, nc.gpsimd)
+                if g + 3 < NG:
+                    load_acts(g + 3)
+                if g + 2 < NG:
+                    load_ig(g + 2)
+                nc.sync.dma_start(out=rows(out_1, g - 1), in_=c_sb[g - 1][:])
+                nc.sync.dma_start(out=rows(out_0, g - 1), in_=hh_sb[g - 1][:])
+                if g + 1 < NG:
+                    quant(g + 1, 0)
+                    quant(g + 1, 1)
+            for m in range(4):
+                stage_f(g, m)
+            if not last:
+                for t in range(TILES):
+                    stage_o(g, t)
+            else:
+                stage_o(g, 0)
+                stage_o(g, 1)
+                for t in range(TILES):
+                    stage_back(g, t)
+                nc.sync.dma_start(out=rows(out_1, g), in_=c_sb[g][:])
+                stage_h(g, 0, nc.gpsimd)
+                stage_h(g, 1, nc.gpsimd)
+                stage_o(g, 2)
+                stage_o(g, 3)
+                nc.sync.dma_start(out=rows(out_0, g)[:, 0:2, :], in_=hh_sb[g][:, 0:2, :])
+                stage_h(g, 2, nc.vector)
+                stage_h(g, 3, nc.vector)
+                nc.sync.dma_start(out=rows(out_0, g)[:, 2:4, :], in_=hh_sb[g][:, 2:4, :])

@@ -14,24 +14,24 @@ ALU = mybir.AluOpType
 P = 128
 B = 4096
 D = 512
-GROUP = 512
-TILES = GROUP // P
-NG = B // GROUP
 FLOPS = 4 * 2 * B * D * D
 
+SIZES = [512, 512, 512, 512, 512, 512, 512, 512]
+NG = len(SIZES)
 S_COLS = 160
+STORE_TILES = 2
+H_ON_V = {NG - 1: 1}
 
 
 def tile_lstmmirrored_pb_t_kernel(
     tc, x, hist, ig, carousel, Wfx, Wfh, b_f, Wox, Woh, b_o, out_0, out_1
 ):
     nc = tc.nc
+    first = [sum(SIZES[:g]) // P for g in range(NG)]
+    ntile = [r // P for r in SIZES]
     with ExitStack() as ctx:
         ctx.enter_context(tc.manual_schedule())
         const = ctx.enter_context(tc.tile_pool(name="const", bufs=1))
-        wstage = ctx.enter_context(tc.tile_pool(name="wstage", bufs=1))
-        acts = ctx.enter_context(tc.tile_pool(name="acts", bufs=4))
-        igp = ctx.enter_context(tc.tile_pool(name="igp", bufs=5))
         work = ctx.enter_context(tc.tile_pool(name="work", bufs=2))
         outp = ctx.enter_context(tc.tile_pool(name="outp", bufs=3))
         psum = ctx.enter_context(tc.psum_pool(name="psum", bufs=8))
@@ -40,32 +40,26 @@ def tile_lstmmirrored_pb_t_kernel(
             return psum.tile([P, 512], F32, name=name, tag="bank")
 
         def rows(ap, g):
-            return ap[g * GROUP : (g + 1) * GROUP, :].rearrange("(p t) d -> p t d", t=TILES)
+            return ap[first[g] * P : (first[g] + ntile[g]) * P, :].rearrange(
+                "(p t) d -> p t d", t=ntile[g]
+            )
 
-        x_sb = {}
-        h_sb = {}
-        ig_sb = {}
+        def mine(tile_ap, g):
+            return tile_ap[:, first[g] : first[g] + ntile[g], :]
 
-        def load_acts(g):
-            x_sb[g] = acts.tile([P, TILES, D], BF16, name="x_sb", tag="x")
-            nc.sync.dma_start(out=x_sb[g][:], in_=rows(x, g))
-            h_sb[g] = acts.tile([P, TILES, D], BF16, name="h_sb", tag="h")
-            nc.sync.dma_start(out=h_sb[g][:], in_=rows(hist, g))
-
-        def load_ig(g):
-            ig_sb[g] = igp.tile([P, TILES, D], BF16, name="ig_sb", tag="ig")
-            nc.sync.dma_start(out=ig_sb[g][:], in_=rows(ig, g))
+        x_all = const.tile([P, B // P, D], BF16, name="x_all")
+        h_all = const.tile([P, B // P, D], BF16, name="h_all")
+        ig_all = const.tile([P, B // P, D], BF16, name="ig_all")
 
         weights = [Wfx, Wfh, Wox, Woh]
-        wraw = []
+        wst = {}
 
         def load_w(w):
-            t = wstage.tile([P, 4, D], BF16, name="wraw%d" % w)
+            wst[w] = outp.tile([P, 2, 4 * D], BF16, name="wst", tag=("c", "c", "c", "hh")[w], align_bytes=64)
             nc.sync.dma_start(
-                out=t[:].rearrange("p (u e) c -> p u e c", u=2),
+                out=wst[w][:, 0, :].rearrange("p (u e c) -> p u e c", u=2, e=2),
                 in_=weights[w].rearrange("(u q e) c -> q u e c", u=2, e=2),
             )
-            wraw.append(t)
 
         ones = const.tile([P, P], BF16, name="ones")
         nc.vector.memset(ones[:], 1.0)
@@ -86,57 +80,49 @@ def tile_lstmmirrored_pb_t_kernel(
         ident_bf = const.tile([P, P], BF16, name="ident_bf")
         make_identity(nc, ident_bf[:])
 
+        def load(tile_ap, src, g):
+            nc.sync.dma_start(out=mine(tile_ap, g), in_=rows(src, g))
+
+        load(x_all, x, 0)
+        load(h_all, hist, 0)
         load_w(0)
         load_w(1)
-        load_acts(0)
+        load(x_all, x, 1)
+        load(h_all, hist, 1)
         load_w(2)
         load_w(3)
-        load_acts(1)
-        load_ig(0)
-        load_acts(2)
-        load_ig(1)
-        load_acts(3)
-        load_ig(2)
-
-        bo_ps = bank("bo_ps")
-        nc.tensor.matmul(out=bo_ps[:], lhsT=ones[:], rhs=brow[:], start=True, stop=True)
-        bf_ps = bank("bf_ps")
-        nc.tensor.matmul(out=bf_ps[:, 0:32], lhsT=bft[:], rhs=ident_bf[:, 0:32], start=True, stop=True)
+        for g in range(2, NG):
+            load(x_all, x, g)
+            load(h_all, hist, g)
+            load(ig_all, ig, g - 2)
+        load(ig_all, ig, NG - 2)
+        load(ig_all, ig, NG - 1)
 
         wcodes = const.tile([P, 4, D], U32, name="wcodes", align_bytes=64)
         wscales = const.tile([P, 4, D], U8, name="wscales", align_bytes=64)
-        wgrp = {}
 
-        def regroup_w(w, s_cols):
-            wgrp[w] = wstage.tile([P, D, 4], BF16, name="wgrp%d" % w, align_bytes=64)
-            v_cols = D - s_cols
-            nc.vector.tensor_copy(
-                out=wgrp[w][:, 0:v_cols, :].rearrange("p (c i) t -> p c t i", i=4),
-                in_=wraw[w][:, :, 0:v_cols].rearrange("p t (c i) -> p c t i", i=4),
+        def regroup_w(w, copy, c0, c1):
+            raw = wst[w][:, 0, :].rearrange("p (t c) -> p t c", t=4)
+            grouped = wst[w][:, 1, :].rearrange("p (c t) -> p c t", t=4)
+            copy(
+                out=grouped[:, c0:c1, :].rearrange("p (c i) t -> p c t i", i=4),
+                in_=raw[:, :, c0:c1].rearrange("p t (c i) -> p c t i", i=4),
             )
-            if s_cols:
-                nc.scalar.copy(
-                    out=wgrp[w][:, v_cols:D, :].rearrange("p (c i) t -> p c t i", i=4),
-                    in_=wraw[w][:, :, v_cols:D].rearrange("p t (c i) -> p c t i", i=4),
-                )
+
+        def regroup_v(w):
+            regroup_w(w, nc.vector.tensor_copy, 0, D - S_COLS)
+
+        def regroup_s(w):
+            regroup_w(w, nc.scalar.copy, D - S_COLS, D)
 
         def quant_w(w):
             nc.vector.quantize_mx(
-                out=wcodes[:, w, :].bitcast(FP8X4),
-                scales=wscales[:, w, :],
-                in_=wgrp[w][:].rearrange("p c t -> p (c t)"),
+                out=wcodes[:, w, :].bitcast(FP8X4), scales=wscales[:, w, :], in_=wst[w][:, 1, :]
             )
 
         bo_bc = const.tile([P, D], F32, name="bo_bc")
         bf_col = const.tile([P, 4], F32, name="bf_col")
         car = const.tile([P, 1], F32, name="car")
-
-        regroup_w(0, S_COLS)
-        nc.vector.tensor_copy(out=bo_bc[:], in_=bo_ps[:])
-        nc.vector.tensor_copy(out=bf_col[:], in_=bf_ps[:, 0:4])
-        nc.vector.tensor_copy(out=car[:], in_=car_bf[:])
-        quant_w(0)
-        regroup_w(1, S_COLS)
 
         grp = {}
         codes = {}
@@ -146,45 +132,48 @@ def tile_lstmmirrored_pb_t_kernel(
         c_sb = {}
         hh_sb = {}
 
+        def in_banks(g):
+            return 2 * max(1, SIZES[g] // 256)
+
         def stage_in(g, k):
-            op, j = k // 2, k % 2
+            per_op = in_banks(g) // 2
+            op, j = k // per_op, k % per_op
+            n = min(SIZES[g], 256)
             if k == 0:
-                grp[g] = work.tile([P, 2, 4 * GROUP], BF16, name="grp", tag="grp", align_bytes=64)
-            src = (x_sb[g], h_sb[g])[op]
+                grp[g] = work.tile([P, 2, 4 * SIZES[g]], BF16, name="grp", tag="grp", align_bytes=64)
+            src = mine((x_all, h_all)[op], g)
             ps = bank("in_ps")
-            for tt in range(2):
-                words = src[:, 2 * j + tt, :].bitcast(F32)
+            for tt in range(n // P):
+                words = src[:, (n // P) * j + tt, :].bitcast(F32)
                 for u in range(2):
                     nc.tensor.transpose(
-                        out=ps[:, u * 256 + tt * P : u * 256 + (tt + 1) * P],
+                        out=ps[:, u * n + tt * P : u * n + (tt + 1) * P],
                         in_=words[:, u * P : (u + 1) * P],
                         identity=ident[:],
                     )
             nc.scalar.copy(
-                out=grp[g][:, op, :].bitcast(F32)[:, j * 512 : (j + 1) * 512].rearrange(
+                out=grp[g][:, op, :].bitcast(F32)[:, j * 2 * n : (j + 1) * 2 * n].rearrange(
                     "p (n u) -> p n u", u=2
                 ),
-                in_=ps[:].rearrange("p (u n) -> p n u", u=2),
+                in_=ps[:, 0 : 2 * n].rearrange("p (u n) -> p n u", u=2),
             )
 
         def quant(g, op):
             if op == 0:
-                codes[g] = work.tile([P, 2, GROUP], U32, name="codes", tag="codes", align_bytes=64)
-                scales[g] = work.tile([P, 2, GROUP], U8, name="scales", tag="scales", align_bytes=64)
+                codes[g] = work.tile([P, 2, SIZES[g]], U32, name="codes", tag="codes", bufs=3, align_bytes=64)
+                scales[g] = work.tile([P, 2, SIZES[g]], U8, name="scales", tag="scales", bufs=3, align_bytes=64)
             nc.vector.quantize_mx(
-                out=codes[g][:, op, :].bitcast(FP8X4),
-                scales=scales[g][:, op, :],
-                in_=grp[g][:, op, :],
+                out=codes[g][:, op, :].bitcast(FP8X4), scales=scales[g][:, op, :], in_=grp[g][:, op, :]
             )
 
         def stage_f(g, m):
             if m == 0:
-                fT[g] = work.tile([P, 4, GROUP], F32, name="fT", tag="fT")
+                fT[g] = work.tile([P, 4, SIZES[g]], F32, name="fT", tag="fT")
             ps = bank("f_ps")
             cols = slice(m * P, (m + 1) * P)
             for op in range(2):
                 nc.tensor.matmul_mx(
-                    out=ps[:],
+                    out=ps[:, 0 : SIZES[g]],
                     lhsT=wcodes[:, op, cols].bitcast(FP8X4),
                     lhsT_scale=wscales[:, op, cols],
                     rhs=codes[g][:, op, :].bitcast(FP8X4),
@@ -193,12 +182,12 @@ def tile_lstmmirrored_pb_t_kernel(
                     stop=(op == 1),
                 )
             nc.scalar.activation(
-                out=fT[g][:, m, :], in_=ps[:], func=ACT.Sigmoid, bias=bf_col[:, m : m + 1], scale=1.0
+                out=fT[g][:, m, :], in_=ps[:, 0 : SIZES[g]], func=ACT.Sigmoid, bias=bf_col[:, m : m + 1], scale=1.0
             )
 
         def stage_o(g, t):
             if t == 0:
-                o_sb[g] = work.tile([P, TILES, D], F32, name="o_sb", tag="o")
+                o_sb[g] = work.tile([P, ntile[g], D], F32, name="o_sb", tag="o")
             ps = bank("o_ps")
             cols = slice(t * P, (t + 1) * P)
             for op in range(2):
@@ -216,8 +205,7 @@ def tile_lstmmirrored_pb_t_kernel(
 
         def stage_back(g, t):
             if t == 0:
-                c_sb[g] = outp.tile([P, TILES, D], F32, name="c_sb", tag="c")
-                hh_sb[g] = outp.tile([P, TILES, D], F32, name="hh_sb", tag="hh")
+                c_sb[g] = outp.tile([P, ntile[g], D], F32, name="c_sb", tag="c", align_bytes=64)
             ps = bank("b_ps")
             for m in range(4):
                 nc.tensor.transpose(
@@ -229,65 +217,78 @@ def tile_lstmmirrored_pb_t_kernel(
                 out=c_sb[g][:, t, :],
                 in0=ps[:],
                 scalar=car[:, 0:1],
-                in1=ig_sb[g][:, t, :],
+                in1=mine(ig_all, g)[:, t, :],
                 op0=ALU.mult,
                 op1=ALU.add,
             )
 
-        def stage_h(g, t, eng):
+        def stage_h(g, t):
+            if t == 0:
+                hh_sb[g] = outp.tile([P, ntile[g], D], F32, name="hh_sb", tag="hh", align_bytes=64)
+            eng = nc.vector if t >= ntile[g] - H_ON_V.get(g, 0) else nc.gpsimd
             eng.tensor_tensor(
                 out=hh_sb[g][:, t, :], in0=o_sb[g][:, t, :], in1=c_sb[g][:, t, :], op=ALU.mult
             )
 
-        for g in range(NG):
-            last = g == NG - 1
-            if g == 0:
-                for k in range(4):
-                    stage_in(0, k)
-                    if k == 1:
-                        quant_w(1)
-                        quant(0, 0)
-                        regroup_w(2, 0)
-                quant(0, 1)
-                quant_w(2)
-                regroup_w(3, 0)
-                quant_w(3)
-            else:
-                if g == 1:
-                    for k in range(4):
-                        stage_in(1, k)
-                    quant(1, 0)
-                    quant(1, 1)
-                for k in range(4):
-                    if g + 1 < NG:
-                        stage_in(g + 1, k)
-                    stage_back(g - 1, k)
-                    stage_h(g - 1, k, nc.gpsimd)
-                if g + 3 < NG:
-                    load_acts(g + 3)
-                if g + 2 < NG:
-                    load_ig(g + 2)
-                nc.sync.dma_start(out=rows(out_1, g - 1), in_=c_sb[g - 1][:])
-                nc.sync.dma_start(out=rows(out_0, g - 1), in_=hh_sb[g - 1][:])
-                if g + 1 < NG:
-                    quant(g + 1, 0)
-                    quant(g + 1, 1)
-            for m in range(4):
-                stage_f(g, m)
-            if not last:
-                for t in range(TILES):
-                    stage_o(g, t)
-            else:
-                stage_o(g, 0)
-                stage_o(g, 1)
-                for t in range(TILES):
-                    stage_back(g, t)
-                nc.sync.dma_start(out=rows(out_1, g), in_=c_sb[g][:])
-                stage_h(g, 0, nc.gpsimd)
-                stage_h(g, 1, nc.gpsimd)
-                stage_o(g, 2)
-                stage_o(g, 3)
-                nc.sync.dma_start(out=rows(out_0, g)[:, 0:2, :], in_=hh_sb[g][:, 0:2, :])
-                stage_h(g, 2, nc.vector)
-                stage_h(g, 3, nc.vector)
-                nc.sync.dma_start(out=rows(out_0, g)[:, 2:4, :], in_=hh_sb[g][:, 2:4, :])
+        def store(kind, g, t):
+            step = 1 if g == NG - 1 else STORE_TILES
+            if (t + 1) % step == 0 or t == ntile[g] - 1:
+                a = t - t % step
+                dst, src = ((out_1, c_sb), (out_0, hh_sb))[kind]
+                nc.sync.dma_start(out=rows(dst, g)[:, a : t + 1, :], in_=src[g][:, a : t + 1, :])
+
+        for k in range(in_banks(0)):
+            stage_in(0, k)
+        quant(0, 0)
+        regroup_v(0)
+        regroup_s(0)
+        quant(0, 1)
+        regroup_v(1)
+        regroup_s(1)
+        quant_w(0)
+        quant_w(1)
+
+        for i in range(NG + 1):
+            ins = [(i + 1, k) for k in range(in_banks(i + 1))] if i + 1 < NG else []
+            backs = [(i - 1, t) for t in range(ntile[i - 1])] if i >= 1 else []
+            for k in range(max(len(ins), len(backs))):
+                if k < len(ins):
+                    stage_in(ins[k][0], ins[k][1])
+                if k < len(backs):
+                    stage_back(i - 1, k)
+                    store(0, i - 1, k)
+                    if i - 1 >= 1:
+                        stage_h(i - 1, k)
+                        store(1, i - 1, k)
+            if i == 0:
+                bo_ps = bank("bo_ps")
+                nc.tensor.matmul(out=bo_ps[:], lhsT=ones[:], rhs=brow[:], start=True, stop=True)
+                bf_ps = bank("bf_ps")
+                nc.tensor.matmul(out=bf_ps[:, 0:32], lhsT=bft[:], rhs=ident_bf[:, 0:32], start=True, stop=True)
+                quant(1, 0)
+                nc.vector.tensor_copy(out=bf_col[:], in_=bf_ps[:, 0:4])
+                regroup_v(2)
+                quant(1, 1)
+                regroup_v(3)
+                nc.vector.tensor_copy(out=car[:], in_=car_bf[:])
+                nc.vector.tensor_copy(out=bo_bc[:], in_=bo_ps[:])
+            elif ins:
+                if i == 1:
+                    quant_w(2)
+                    quant_w(3)
+                quant(i + 1, 0)
+                quant(i + 1, 1)
+            if i < NG:
+                for m in range(4):
+                    stage_f(i, m)
+            if i == 0:
+                regroup_s(2)
+                regroup_s(3)
+            if i == 1:
+                for t in range(ntile[0]):
+                    stage_o(0, t)
+                    stage_h(0, t)
+                    store(1, 0, t)
+            if 1 <= i < NG:
+                for t in range(ntile[i]):
+                    stage_o(i, t)

@@ -16,7 +16,7 @@ B = 4096
 D = 512
 FLOPS = 4 * 2 * B * D * D
 
-SIZES = [512, 512, 512, 512, 512, 512, 512, 512]
+SIZES = [512]*8
 NG = len(SIZES)
 S_COLS = 160
 STORE_TILES = 2
@@ -237,8 +237,24 @@ def tile_lstmmirrored_pb_t_kernel(
                 dst, src = ((out_1, c_sb), (out_0, hh_sb))[kind]
                 nc.sync.dma_start(out=rows(dst, g)[:, a : t + 1, :], in_=src[g][:, a : t + 1, :])
 
-        for k in range(in_banks(0)):
-            stage_in(0, k)
+        def in_half(g, op):
+            if g >= NG:
+                return []
+            per_op = in_banks(g) // 2
+            return [(g, op * per_op + k) for k in range(per_op)]
+
+        def tr_run(ins, g, backs):
+            for k in range(max(len(ins), len(backs))):
+                if k < len(ins):
+                    stage_in(ins[k][0], ins[k][1])
+                if k < len(backs):
+                    stage_back(g, backs[k])
+                    store(0, g, backs[k])
+                    if g >= 1:
+                        stage_h(g, backs[k])
+                        store(1, g, backs[k])
+
+        tr_run(in_half(0, 0) + in_half(0, 1), 0, [])
         quant(0, 0)
         regroup_v(0)
         regroup_s(0)
@@ -247,48 +263,42 @@ def tile_lstmmirrored_pb_t_kernel(
         regroup_s(1)
         quant_w(0)
         quant_w(1)
+        tr_run(in_half(1, 0) + in_half(1, 1), 0, [])
+        bo_ps = bank("bo_ps")
+        nc.tensor.matmul(out=bo_ps[:], lhsT=ones[:], rhs=brow[:], start=True, stop=True)
+        bf_ps = bank("bf_ps")
+        nc.tensor.matmul(out=bf_ps[:, 0:32], lhsT=bft[:], rhs=ident_bf[:, 0:32], start=True, stop=True)
+        quant(1, 0)
+        nc.vector.tensor_copy(out=bf_col[:], in_=bf_ps[:, 0:4])
+        regroup_v(2)
+        quant(1, 1)
+        regroup_v(3)
+        nc.vector.tensor_copy(out=car[:], in_=car_bf[:])
+        nc.vector.tensor_copy(out=bo_bc[:], in_=bo_ps[:])
+        for m in range(4):
+            stage_f(0, m)
+        regroup_s(2)
+        regroup_s(3)
+        tr_run(in_half(2, 0), 0, [])
 
-        for i in range(NG + 1):
-            ins = [(i + 1, k) for k in range(in_banks(i + 1))] if i + 1 < NG else []
-            backs = [(i - 1, t) for t in range(ntile[i - 1])] if i >= 1 else []
-            for k in range(max(len(ins), len(backs))):
-                if k < len(ins):
-                    stage_in(ins[k][0], ins[k][1])
-                if k < len(backs):
-                    stage_back(i - 1, k)
-                    store(0, i - 1, k)
-                    if i - 1 >= 1:
-                        stage_h(i - 1, k)
-                        store(1, i - 1, k)
-            if i == 0:
-                bo_ps = bank("bo_ps")
-                nc.tensor.matmul(out=bo_ps[:], lhsT=ones[:], rhs=brow[:], start=True, stop=True)
-                bf_ps = bank("bf_ps")
-                nc.tensor.matmul(out=bf_ps[:, 0:32], lhsT=bft[:], rhs=ident_bf[:, 0:32], start=True, stop=True)
-                quant(1, 0)
-                nc.vector.tensor_copy(out=bf_col[:], in_=bf_ps[:, 0:4])
-                regroup_v(2)
-                quant(1, 1)
-                regroup_v(3)
-                nc.vector.tensor_copy(out=car[:], in_=car_bf[:])
-                nc.vector.tensor_copy(out=bo_bc[:], in_=bo_ps[:])
-            elif ins:
-                if i == 1:
-                    quant_w(2)
-                    quant_w(3)
+        for i in range(1, NG + 1):
+            half = max(1, ntile[i - 1] // 2)
+            tr_run(in_half(i + 1, 1), i - 1, list(range(0, half)))
+            if i == 1:
+                quant_w(2)
+                quant_w(3)
+            if i + 1 < NG:
                 quant(i + 1, 0)
                 quant(i + 1, 1)
             if i < NG:
                 for m in range(4):
                     stage_f(i, m)
-            if i == 0:
-                regroup_s(2)
-                regroup_s(3)
+            tr_run(in_half(i + 2, 0), i - 1, list(range(half, ntile[i - 1])))
             if i == 1:
                 for t in range(ntile[0]):
                     stage_o(0, t)
                     stage_h(0, t)
                     store(1, 0, t)
-            if 1 <= i < NG:
+            if i < NG:
                 for t in range(ntile[i]):
                     stage_o(i, t)

@@ -16,11 +16,12 @@ B = 4096
 D = 512
 FLOPS = 4 * 2 * B * D * D
 
-SIZES = [512]*8
+SIZES = [512] * 8
 NG = len(SIZES)
 S_COLS = 160
 STORE_TILES = 2
-H_ON_V = {NG - 1: 1}
+V_CO = (3,)
+H_ON_V = {NG - 1: 2}
 
 
 def tile_lstmmirrored_pb_t_kernel(
@@ -151,7 +152,8 @@ def tile_lstmmirrored_pb_t_kernel(
                         in_=words[:, u * P : (u + 1) * P],
                         identity=ident[:],
                     )
-            nc.scalar.copy(
+            copy = nc.vector.tensor_copy if (k in V_CO and g >= 2) else nc.scalar.copy
+            copy(
                 out=grp[g][:, op, :].bitcast(F32)[:, j * 2 * n : (j + 1) * 2 * n].rearrange(
                     "p (n u) -> p n u", u=2
                 ),
@@ -250,7 +252,7 @@ def tile_lstmmirrored_pb_t_kernel(
                 if k < len(backs):
                     stage_back(g, backs[k])
                     store(0, g, backs[k])
-                    if g >= 1:
+                    if 1 <= g < NG - 1:
                         stage_h(g, backs[k])
                         store(1, g, backs[k])
 
@@ -302,3 +304,10 @@ def tile_lstmmirrored_pb_t_kernel(
             if i < NG:
                 for t in range(ntile[i]):
                     stage_o(i, t)
+        n_g = ntile[NG - 1] - H_ON_V[NG - 1]
+        for t in range(ntile[NG - 1]):
+            stage_h(NG - 1, t)
+        for k in range(ntile[NG - 1]):
+            for t in (k, n_g + k):
+                if (t < n_g) == (t == k) and t < ntile[NG - 1]:
+                    store(1, NG - 1, t)

@@ -31,7 +31,6 @@ def tile_lstmmirrored_pb_t_kernel(
     first = [sum(SIZES[:g]) // P for g in range(NG)]
     ntile = [r // P for r in SIZES]
     with ExitStack() as ctx:
-        ctx.enter_context(tc.manual_schedule())
         const = ctx.enter_context(tc.tile_pool(name="const", bufs=1))
         work = ctx.enter_context(tc.tile_pool(name="work", bufs=2))
         outp = ctx.enter_context(tc.tile_pool(name="outp", bufs=3))

@@ -21,6 +21,8 @@ NG = len(SIZES)
 S_COLS = 160
 STORE_TILES = 2
 V_CO = (3,)
+N1 = 3
+N2 = 1
 H_ON_V = {NG - 1: 2}
 
 
@@ -31,6 +33,7 @@ def tile_lstmmirrored_pb_t_kernel(
     first = [sum(SIZES[:g]) // P for g in range(NG)]
     ntile = [r // P for r in SIZES]
     with ExitStack() as ctx:
+        ctx.enter_context(tc.manual_schedule())
         const = ctx.enter_context(tc.tile_pool(name="const", bufs=1))
         work = ctx.enter_context(tc.tile_pool(name="work", bufs=2))
         outp = ctx.enter_context(tc.tile_pool(name="outp", bufs=3))
@@ -264,7 +267,16 @@ def tile_lstmmirrored_pb_t_kernel(
         regroup_s(1)
         quant_w(0)
         quant_w(1)
-        tr_run(in_half(1, 0) + in_half(1, 1), 0, [])
+        def spin(n):
+            if n:
+                sp = bank("spin_ps")
+                for k in range(n):
+                    nc.tensor.matmul(out=sp[:], lhsT=ones[:], rhs=brow[:], start=True, stop=True)
+
+        spin(N1)
+        tr_run(in_half(1, 0), 0, [])
+        spin(N2)
+        tr_run(in_half(1, 1), 0, [])
         bo_ps = bank("bo_ps")
         nc.tensor.matmul(out=bo_ps[:], lhsT=ones[:], rhs=brow[:], start=True, stop=True)
         bf_ps = bank("bf_ps")

@@ -19,7 +19,7 @@ FLOPS = 4 * 2 * B * D * D
 SIZES = [512] * 8
 NG = len(SIZES)
 S_COLS = 160
-STORE_TILES = 2
+STORE_TILES = 4
 V_CO = (3,)
 N1 = 3
 N2 = 1
@@ -43,9 +43,7 @@ def tile_lstmmirrored_pb_t_kernel(
             return psum.tile([P, 512], F32, name=name, tag="bank")
 
         def rows(ap, g):
-            return ap[first[g] * P : (first[g] + ntile[g]) * P, :].rearrange(
-                "(p t) d -> p t d", t=ntile[g]
-            )
+            return ap.rearrange("(p t) d -> p t d", t=B // P)[:, first[g] : first[g] + ntile[g], :]
 
         def mine(tile_ap, g):
             return tile_ap[:, first[g] : first[g] + ntile[g], :]
@@ -83,8 +81,11 @@ def tile_lstmmirrored_pb_t_kernel(
         ident_bf = const.tile([P, P], BF16, name="ident_bf")
         make_identity(nc, ident_bf[:])
 
-        def load(tile_ap, src, g):
-            nc.sync.dma_start(out=mine(tile_ap, g), in_=rows(src, g))
+        def load(tile_ap, src, g, n=1):
+            t0, t1 = first[g], first[g + n - 1] + ntile[g + n - 1]
+            nc.sync.dma_start(
+                out=tile_ap[:, t0:t1, :], in_=src.rearrange("(p t) d -> p t d", t=B // P)[:, t0:t1, :]
+            )
 
         load(x_all, x, 0)
         load(h_all, hist, 0)
@@ -94,12 +95,16 @@ def tile_lstmmirrored_pb_t_kernel(
         load(h_all, hist, 1)
         load_w(2)
         load_w(3)
-        for g in range(2, NG):
+        for g in (2, 3):
             load(x_all, x, g)
             load(h_all, hist, g)
             load(ig_all, ig, g - 2)
-        load(ig_all, ig, NG - 2)
-        load(ig_all, ig, NG - 1)
+        load(x_all, x, 4, 2)
+        load(h_all, hist, 4, 2)
+        load(ig_all, ig, 2, 2)
+        load(x_all, x, 6, 2)
+        load(h_all, hist, 6, 2)
+        load(ig_all, ig, 4, 4)
 
         wcodes = const.tile([P, 4, D], U32, name="wcodes", align_bytes=64)
         wscales = const.tile([P, 4, D], U8, name="wscales", align_bytes=64)
@@ -235,7 +240,7 @@ def tile_lstmmirrored_pb_t_kernel(
             )
 
         def store(kind, g, t):
-            step = 1 if g == NG - 1 else STORE_TILES
+            step = 1 if g == NG - 1 else (2 if g == NG - 2 else STORE_TILES)
             if (t + 1) % step == 0 or t == ntile[g] - 1:
                 a = t - t % step
                 dst, src = ((out_1, c_sb), (out_0, hh_sb))[kind]

from contextlib import ExitStack

import concourse.mybir as mybir
from concourse.masks import make_identity

F32 = mybir.dt.float32
BF16 = mybir.dt.bfloat16
U32 = mybir.dt.uint32
U8 = mybir.dt.uint8
FP8X4 = mybir.dt.float8_e4m3fn_x4
ACT = mybir.ActivationFunctionType
ALU = mybir.AluOpType

P = 128
B = 4096
D = 512
FLOPS = 4 * 2 * B * D * D

SIZES = [512] * 8
NG = len(SIZES)
S_COLS = 160
STORE_TILES = 4
V_CO = (3,)
N1 = 3
N2 = 1
H_ON_V = {NG - 1: 2}


def tile_lstmmirrored_pb_t_kernel(
    tc, x, hist, ig, carousel, Wfx, Wfh, b_f, Wox, Woh, b_o, out_0, out_1
):
    nc = tc.nc
    first = [sum(SIZES[:g]) // P for g in range(NG)]
    ntile = [r // P for r in SIZES]
    with ExitStack() as ctx:
        ctx.enter_context(tc.manual_schedule())
        const = ctx.enter_context(tc.tile_pool(name="const", bufs=1))
        work = ctx.enter_context(tc.tile_pool(name="work", bufs=2))
        outp = ctx.enter_context(tc.tile_pool(name="outp", bufs=3))
        psum = ctx.enter_context(tc.psum_pool(name="psum", bufs=8))

        def bank(name):
            return psum.tile([P, 512], F32, name=name, tag="bank")

        def rows(ap, g):
            return ap.rearrange("(p t) d -> p t d", t=B // P)[:, first[g] : first[g] + ntile[g], :]

        def mine(tile_ap, g):
            return tile_ap[:, first[g] : first[g] + ntile[g], :]

        x_all = const.tile([P, B // P, D], BF16, name="x_all")
        h_all = const.tile([P, B // P, D], BF16, name="h_all")
        ig_all = const.tile([P, B // P, D], BF16, name="ig_all")

        weights = [Wfx, Wfh, Wox, Woh]
        wst = {}

        def load_w(w):
            wst[w] = outp.tile([P, 2, 4 * D], BF16, name="wst", tag=("c", "c", "c", "hh")[w], align_bytes=64)
            nc.sync.dma_start(
                out=wst[w][:, 0, :].rearrange("p (u e c) -> p u e c", u=2, e=2),
                in_=weights[w].rearrange("(u q e) c -> q u e c", u=2, e=2),
            )

        ones = const.tile([P, P], BF16, name="ones")
        nc.vector.memset(ones[:], 1.0)
        brow = const.tile([P, D], BF16, name="brow")
        nc.vector.memset(brow[:], 0.0)
        bft = const.tile([P, P], BF16, name="bft")
        nc.vector.memset(bft[:], 0.0)
        warm = const.tile([P, 1], F32, name="warm")
        nc.vector.memset(warm[:], 0.0)
        car_bf = const.tile([P, 1], BF16, name="car_bf")
        nc.scalar.dma_start(out=brow[0:1, :], in_=b_o.unsqueeze(0))
        nc.scalar.dma_start(out=bft[0:4, :], in_=b_f.rearrange("(m d) -> m d", m=4))
        nc.scalar.dma_start(out=car_bf[:], in_=carousel.partition_broadcast(P))
        nc.scalar.activation(out=warm[:], in_=warm[:], func=ACT.Sigmoid)

        ident = const.tile([P, P], F32, name="ident")
        make_identity(nc, ident[:])
        ident_bf = const.tile([P, P], BF16, name="ident_bf")
        make_identity(nc, ident_bf[:])

        def load(tile_ap, src, g, n=1):
            t0, t1 = first[g], first[g + n - 1] + ntile[g + n - 1]
            nc.sync.dma_start(
                out=tile_ap[:, t0:t1, :], in_=src.rearrange("(p t) d -> p t d", t=B // P)[:, t0:t1, :]
            )

        load(x_all, x, 0)
        load(h_all, hist, 0)
        load_w(0)
        load_w(1)
        load(x_all, x, 1)
        load(h_all, hist, 1)
        load_w(2)
        load_w(3)
        for g in (2, 3):
            load(x_all, x, g)
            load(h_all, hist, g)
            load(ig_all, ig, g - 2)
        load(x_all, x, 4, 2)
        load(h_all, hist, 4, 2)
        load(ig_all, ig, 2, 2)
        load(x_all, x, 6, 2)
        load(h_all, hist, 6, 2)
        load(ig_all, ig, 4, 4)

        wcodes = const.tile([P, 4, D], U32, name="wcodes", align_bytes=64)
        wscales = const.tile([P, 4, D], U8, name="wscales", align_bytes=64)

        def regroup_w(w, copy, c0, c1):
            raw = wst[w][:, 0, :].rearrange("p (t c) -> p t c", t=4)
            grouped = wst[w][:, 1, :].rearrange("p (c t) -> p c t", t=4)
            copy(
                out=grouped[:, c0:c1, :].rearrange("p (c i) t -> p c t i", i=4),
                in_=raw[:, :, c0:c1].rearrange("p t (c i) -> p c t i", i=4),
            )

        def regroup_v(w):
            regroup_w(w, nc.vector.tensor_copy, 0, D - S_COLS)

        def regroup_s(w):
            regroup_w(w, nc.scalar.copy, D - S_COLS, D)

        def quant_w(w):
            nc.vector.quantize_mx(
                out=wcodes[:, w, :].bitcast(FP8X4), scales=wscales[:, w, :], in_=wst[w][:, 1, :]
            )

        bo_bc = const.tile([P, D], F32, name="bo_bc")
        bf_col = const.tile([P, 4], F32, name="bf_col")
        car = const.tile([P, 1], F32, name="car")

        grp = {}
        codes = {}
        scales = {}
        fT = {}
        o_sb = {}
        c_sb = {}
        hh_sb = {}

        def in_banks(g):
            return 2 * max(1, SIZES[g] // 256)

        def stage_in(g, k):
            per_op = in_banks(g) // 2
            op, j = k // per_op, k % per_op
            n = min(SIZES[g], 256)
            if k == 0:
                grp[g] = work.tile([P, 2, 4 * SIZES[g]], BF16, name="grp", tag="grp", align_bytes=64)
            src = mine((x_all, h_all)[op], g)
            ps = bank("in_ps")
            for tt in range(n // P):
                words = src[:, (n // P) * j + tt, :].bitcast(F32)
                for u in range(2):
                    nc.tensor.transpose(
                        out=ps[:, u * n + tt * P : u * n + (tt + 1) * P],
                        in_=words[:, u * P : (u + 1) * P],
                        identity=ident[:],
                    )
            copy = nc.vector.tensor_copy if (k in V_CO and g >= 2) else nc.scalar.copy
            copy(
                out=grp[g][:, op, :].bitcast(F32)[:, j * 2 * n : (j + 1) * 2 * n].rearrange(
                    "p (n u) -> p n u", u=2
                ),
                in_=ps[:, 0 : 2 * n].rearrange("p (u n) -> p n u", u=2),
            )

        def quant(g, op):
            if op == 0:
                codes[g] = work.tile([P, 2, SIZES[g]], U32, name="codes", tag="codes", bufs=3, align_bytes=64)
                scales[g] = work.tile([P, 2, SIZES[g]], U8, name="scales", tag="scales", bufs=3, align_bytes=64)
            nc.vector.quantize_mx(
                out=codes[g][:, op, :].bitcast(FP8X4), scales=scales[g][:, op, :], in_=grp[g][:, op, :]
            )

        def stage_f(g, m):
            if m == 0:
                fT[g] = work.tile([P, 4, SIZES[g]], F32, name="fT", tag="fT")
            ps = bank("f_ps")
            cols = slice(m * P, (m + 1) * P)
            for op in range(2):
                nc.tensor.matmul_mx(
                    out=ps[:, 0 : SIZES[g]],
                    lhsT=wcodes[:, op, cols].bitcast(FP8X4),
                    lhsT_scale=wscales[:, op, cols],
                    rhs=codes[g][:, op, :].bitcast(FP8X4),
                    rhs_scale=scales[g][:, op, :],
                    start=(op == 0),
                    stop=(op == 1),
                )
            nc.scalar.activation(
                out=fT[g][:, m, :], in_=ps[:, 0 : SIZES[g]], func=ACT.Sigmoid, bias=bf_col[:, m : m + 1], scale=1.0
            )

        def stage_o(g, t):
            if t == 0:
                o_sb[g] = work.tile([P, ntile[g], D], F32, name="o_sb", tag="o")
            ps = bank("o_ps")
            cols = slice(t * P, (t + 1) * P)
            for op in range(2):
                nc.tensor.matmul_mx(
                    out=ps[:],
                    lhsT=codes[g][:, op, cols].bitcast(FP8X4),
                    lhsT_scale=scales[g][:, op, cols],
                    rhs=wcodes[:, 2 + op, :].bitcast(FP8X4),
                    rhs_scale=wscales[:, 2 + op, :],
                    start=(op == 0),
                    stop=(op == 1),
                )
            nc.vector.tensor_tensor(out=o_sb[g][:, t, :], in0=ps[:], in1=bo_bc[:], op=ALU.add)
            nc.scalar.activation(out=o_sb[g][:, t, :], in_=o_sb[g][:, t, :], func=ACT.Sigmoid)

        def stage_back(g, t):
            if t == 0:
                c_sb[g] = outp.tile([P, ntile[g], D], F32, name="c_sb", tag="c", align_bytes=64)
            ps = bank("b_ps")
            for m in range(4):
                nc.tensor.transpose(
                    out=ps[:, m * P : (m + 1) * P],
                    in_=fT[g][:, m, t * P : (t + 1) * P],
                    identity=ident[:],
                )
            nc.vector.scalar_tensor_tensor(
                out=c_sb[g][:, t, :],
                in0=ps[:],
                scalar=car[:, 0:1],
                in1=mine(ig_all, g)[:, t, :],
                op0=ALU.mult,
                op1=ALU.add,
            )

        def stage_h(g, t):
            if t == 0:
                hh_sb[g] = outp.tile([P, ntile[g], D], F32, name="hh_sb", tag="hh", align_bytes=64)
            eng = nc.vector if t >= ntile[g] - H_ON_V.get(g, 0) else nc.gpsimd
            eng.tensor_tensor(
                out=hh_sb[g][:, t, :], in0=o_sb[g][:, t, :], in1=c_sb[g][:, t, :], op=ALU.mult
            )

        def store(kind, g, t):
            step = 1 if g == NG - 1 else (2 if g == NG - 2 else STORE_TILES)
            if (t + 1) % step == 0 or t == ntile[g] - 1:
                a = t - t % step
                dst, src = ((out_1, c_sb), (out_0, hh_sb))[kind]
                nc.sync.dma_start(out=rows(dst, g)[:, a : t + 1, :], in_=src[g][:, a : t + 1, :])

        def in_half(g, op):
            if g >= NG:
                return []
            per_op = in_banks(g) // 2
            return [(g, op * per_op + k) for k in range(per_op)]

        def tr_run(ins, g, backs):
            for k in range(max(len(ins), len(backs))):
                if k < len(ins):
                    stage_in(ins[k][0], ins[k][1])
                if k < len(backs):
                    stage_back(g, backs[k])
                    store(0, g, backs[k])
                    if 1 <= g < NG - 1:
                        stage_h(g, backs[k])
                        store(1, g, backs[k])

        tr_run(in_half(0, 0) + in_half(0, 1), 0, [])
        quant(0, 0)
        regroup_v(0)
        regroup_s(0)
        quant(0, 1)
        regroup_v(1)
        regroup_s(1)
        quant_w(0)
        quant_w(1)
        def spin(n):
            if n:
                sp = bank("spin_ps")
                for k in range(n):
                    nc.tensor.matmul(out=sp[:], lhsT=ones[:], rhs=brow[:], start=True, stop=True)

        spin(N1)
        tr_run(in_half(1, 0), 0, [])
        spin(N2)
        tr_run(in_half(1, 1), 0, [])
        bo_ps = bank("bo_ps")
        nc.tensor.matmul(out=bo_ps[:], lhsT=ones[:], rhs=brow[:], start=True, stop=True)
        bf_ps = bank("bf_ps")
        nc.tensor.matmul(out=bf_ps[:, 0:32], lhsT=bft[:], rhs=ident_bf[:, 0:32], start=True, stop=True)
        quant(1, 0)
        nc.vector.tensor_copy(out=bf_col[:], in_=bf_ps[:, 0:4])
        regroup_v(2)
        quant(1, 1)
        regroup_v(3)
        nc.vector.tensor_copy(out=car[:], in_=car_bf[:])
        nc.vector.tensor_copy(out=bo_bc[:], in_=bo_ps[:])
        for m in range(4):
            stage_f(0, m)
        regroup_s(2)
        regroup_s(3)
        tr_run(in_half(2, 0), 0, [])

        for i in range(1, NG + 1):
            half = max(1, ntile[i - 1] // 2)
            tr_run(in_half(i + 1, 1), i - 1, list(range(0, half)))
            if i == 1:
                quant_w(2)
                quant_w(3)
            if i + 1 < NG:
                quant(i + 1, 0)
                quant(i + 1, 1)
            if i < NG:
                for m in range(4):
                    stage_f(i, m)
            tr_run(in_half(i + 2, 0), i - 1, list(range(half, ntile[i - 1])))
            if i == 1:
                for t in range(ntile[0]):
                    stage_o(0, t)
                    stage_h(0, t)
                    store(1, 0, t)
            if i < NG:
                for t in range(ntile[i]):
                    stage_o(i, t)
        n_g = ntile[NG - 1] - H_ON_V[NG - 1]
        for t in range(ntile[NG - 1]):
            stage_h(NG - 1, t)
        for k in range(ntile[NG - 1]):
            for t in (k, n_g + k):
                if (t < n_g) == (t == k) and t < ntile[NG - 1]:
                    store(1, NG - 1, t)
